import numpy as np
import ml_dtypes


def mxq(x, axis, fmt="e4m3"):
    dtype, down = {"e4m3": (ml_dtypes.float8_e4m3fn, 7), "e5m2": (ml_dtypes.float8_e5m2, 14)}[fmt]
    v = np.moveaxis(np.asarray(x, np.float32).astype(ml_dtypes.bfloat16).astype(np.float64), axis, -1)
    blocks = v.reshape(v.shape[:-1] + (-1, 32))
    amax = np.abs(blocks).max(-1, keepdims=True)
    byte = np.maximum(np.where(amax > 0, np.frexp(amax)[1] - 1 + 127, 0) - down, 1)
    scale = np.exp2(byte - 127.0)
    codes = (blocks / scale).astype(np.float32).astype(dtype).astype(np.float64)
    return np.moveaxis((codes * scale).reshape(v.shape), -1, axis)


WIDE = False


def mx_kscale(k):
    if not WIDE:
        return np.ones(k)
    levels = np.array([10, -10, 5, -5, 0])
    a = np.random.permutation(np.resize(levels, k // 512 * 4)).reshape(k // 512, 4)
    idx = np.arange(k)
    return np.exp2(a[idx // 512, idx % 128 // 32])


BF16 = ml_dtypes.bfloat16


def bf(x):
    return np.asarray(x, np.float32).astype(BF16)


def f64(x):
    return np.asarray(x).astype(np.float64)


B, S, L, H = 2, 16, 8, 512
F = 2 * H
VERT = np.array([[-1, -1, -1], [-1, -1, 1], [-1, 1, -1], [-1, 1, 1], [1, -1, -1], [1, -1, 1], [1, 1, -1], [1, 1, 1]], np.float64) * (np.pi / 2)


def sigmoid(v):
    return 1.0 / (1.0 + np.exp(-v))


def routing_matrix(p, t):
    mid = (p[:, None, :] + p[None, :, :]) * 0.5
    cx, cy, cz = mid[..., 0], mid[..., 1], mid[..., 2]
    f = (np.sin(cx) * np.cos(cy) + np.sin(cy) * np.cos(cz) + np.sin(cz) * np.cos(cx)) - t
    r = sigmoid(2.0 * f)
    r = np.where(np.eye(L) > 0, 1.0, r)
    return r / (r.sum(axis=1, keepdims=True) + 1e-6)


def setup_inputs():
    s = mx_kscale(H)
    return {"x": bf(np.random.standard_normal((B, S, L, H)) * s),
            "limb_positions": bf(VERT + 0.2 * np.random.standard_normal(VERT.shape)),
            "channel_threshold": bf(np.atleast_1d(0.3 + 0.1 * np.random.standard_normal())),
            "W_route": bf(np.random.standard_normal((H, H)) * 2.0 / np.sqrt(H) * s[:, None] / s[None, :]),
            "b_route": bf(np.random.standard_normal(H) * 0.5 * s),
            "W_gate": bf(np.random.standard_normal((H, F)) / np.sqrt(H) / np.concatenate([s, s])[None, :]),
            "b_gate": bf(np.random.standard_normal(H) * 0.5)}


def reference(x, limb_positions, channel_threshold, W_route, b_route, W_gate, b_gate):
    x = f64(x)
    routing = routing_matrix(f64(limb_positions), f64(channel_threshold))
    xq = mxq(x, 3, "e4m3")
    projected = (xq @ mxq(f64(W_route), 1, "e4m3").T) + f64(b_route)
    routed = sum(routing[:, j][None, None, :, None] * projected[:, :, j:j + 1, :] for j in range(L))
    gate_in = np.concatenate([xq, mxq(routed, 3, "e4m3")], axis=-1)
    gate = sigmoid((gate_in @ mxq(f64(W_gate), 1, "e4m3").T) + f64(b_gate))
    return gate * routed + (1.0 - gate) * x

@@ -1,0 +1,355 @@
+import math
+from contextlib import ExitStack
+
+import concourse.mybir as mybir
+from concourse.masks import make_identity
+
+F32 = mybir.dt.float32
+BF16 = mybir.dt.bfloat16
+U32 = mybir.dt.uint32
+U8 = mybir.dt.uint8
+FP8X4 = mybir.dt.float8_e4m3fn_x4
+ALU = mybir.AluOpType
+ACT = mybir.ActivationFunctionType
+AXIS_X = mybir.AxisListType.X
+
+P = 128
+TOKENS = 256
+TOKEN_TILES = TOKENS // P
+LIMBS = 8
+GROUPS = P // LIMBS
+COORDS = 3
+H = 512
+SLOTS = 4
+BANK = 512
+HALF = BANK // 2
+ROUND_MAGIC = 1.5 * 2.0**23
+
+FLOPS = 2 * TOKENS * H * H + 2 * TOKENS * 2 * H * H + 2 * TOKENS * LIMBS * H
+
+
+def transpose_and_group(nc, psum, ident, row_blocks, grouped, on_scalar):
+    bank = psum.tile([P, 2, HALF], F32, tag="bank", name="words_t")
+    for b, rows in enumerate(row_blocks):
+        words = rows.bitcast(F32)
+        for u in range(2):
+            nc.tensor.transpose(bank[:, u, b * P : (b + 1) * P], words[:, u * P : (u + 1) * P], ident)
+    interleaved = bank[:].rearrange("q u c -> q c u")
+    if on_scalar:
+        nc.scalar.copy(out=grouped.bitcast(F32), in_=interleaved)
+    else:
+        nc.vector.tensor_copy(out=grouped.bitcast(F32), in_=interleaved)
+
+
+def quantise(nc, grouped, codes, scales):
+    nc.vector.quantize_mx(out=codes.bitcast(FP8X4), scales=scales, in_=grouped.rearrange("q c s -> q (c s)"))
+
+
+def tile_tpmslimbrouter_pa_s_kernel(
+    tc, x, limb_positions, channel_threshold, W_route, b_route, W_gate, b_gate, out
+):
+    nc = tc.nc
+    x_rows = x.flatten_outer_dims()
+    out_rows = out.flatten_outer_dims()
+
+    with ExitStack() as ctx:
+        keep = ctx.enter_context(tc.tile_pool(name="keep", bufs=1))
+        psum = ctx.enter_context(tc.psum_pool(name="psum", bufs=8))
+        ctx.enter_context(tc.manual_schedule())
+
+        ident = keep.tile([P, P], F32, name="ident")
+        make_identity(nc, ident[:])
+        ones = keep.tile([P, P], BF16, name="ones")
+        nc.gpsimd.memset(ones[:], 1.0)
+        smalls = keep.tile([P, 64], BF16, name="smalls")
+        nc.vector.memset(smalls[:], 0.0)
+        warm = keep.tile([P, 1], F32, name="warm")
+        nc.vector.memset(warm[:], 0.0)
+
+        THR = 32
+        nc.scalar.dma_start(
+            out=smalls[0:1, 0 : LIMBS * COORDS], in_=limb_positions.rearrange("i c -> (i c)").unsqueeze(0)
+        )
+        nc.scalar.dma_start(out=smalls[0:1, THR : THR + 1], in_=channel_threshold.unsqueeze(0))
+        b_route_bf = keep.tile([P, 2, 2], BF16, name="b_route_bf")
+        nc.scalar.dma_start(out=b_route_bf[:], in_=b_route.rearrange("(u q e) -> q u e", u=2, e=2))
+        b_gate_bf = keep.tile([P, 2, 2], BF16, name="b_gate_bf")
+        nc.scalar.dma_start(out=b_gate_bf[:], in_=b_gate.rearrange("(u q e) -> q u e", u=2, e=2))
+
+        x_sb = keep.tile([P, TOKEN_TILES, H], BF16, name="x_sb")
+        nc.sync.dma_start(out=x_sb[:], in_=x_rows.rearrange("(n p) k -> p n k", p=P))
+        wr_sb = keep.tile([P, SLOTS, H], BF16, name="wr_sb")
+        wg_sb = keep.tile([P, SLOTS, 2 * H], BF16, name="wg_sb")
+        for w_sb, w in ((wr_sb, W_route), (wg_sb, W_gate)):
+            for u in range(2):
+                nc.sync.dma_start(
+                    out=w_sb[:, 2 * u : 2 * u + 2, :],
+                    in_=w[256 * u : 256 * (u + 1), :].rearrange("(q e) k -> q e k", e=2),
+                )
+
+        nc.scalar.activation(out=warm[:], in_=warm[:], func=ACT.Silu)
+
+        own_limb = keep.tile([P, LIMBS], F32, name="own_limb")
+        nc.vector.tensor_reduce(
+            out=own_limb[:], in_=ident[:].rearrange("p (a j) -> p j a", j=LIMBS), axis=AXIS_X, op=ALU.add
+        )
+        own_group = keep.tile([P, GROUPS], F32, name="own_group")
+        nc.vector.tensor_reduce(
+            out=own_group[:], in_=ident[:].rearrange("p (a j) -> p a j", j=LIMBS), axis=AXIS_X, op=ALU.add
+        )
+        PAIRS = 1 + LIMBS
+        diag_flat = keep.tile([P, LIMBS * (PAIRS + 1)], F32, name="diag_flat")
+        nc.vector.memset(diag_flat[:], 0.0)
+        nc.vector.memset(diag_flat[:].rearrange("p (i s) -> p i s", s=PAIRS + 1)[:, :, 1], 2.0)
+        two_on_diag = diag_flat[:, 0 : LIMBS * PAIRS].rearrange("p (i s) -> p i s", s=PAIRS)
+        nc.vector.tensor_scalar(out=two_on_diag[:, :, 0], in0=own_limb[:], scalar1=2.0, scalar2=None, op0=ALU.mult)
+        twice_r = keep.tile([P, LIMBS, PAIRS + 1], F32, name="twice_r")
+        nc.vector.memset(twice_r[:, :, PAIRS], 2.0e-6)
+
+        spread = psum.tile([P, BANK], F32, tag="bank", name="spread")
+        nc.tensor.matmul(out=spread[:, 0:64], lhsT=ones[:], rhs=smalls[:], start=True, stop=True)
+        PLANES = 2 * COORDS
+        positions = spread[:, 0 : LIMBS * COORDS].rearrange("p (i c) -> p i c", c=COORDS)
+        turns = keep.tile([P, LIMBS, PLANES], F32, name="turns")
+        nc.vector.tensor_scalar(
+            out=turns[:, :, 0:COORDS], in0=positions, scalar1=1.0 / (4.0 * math.pi), scalar2=None, op0=ALU.mult
+        )
+        nc.vector.tensor_scalar(
+            out=turns[:, :, COORDS:PLANES],
+            in0=positions,
+            scalar1=1.0 / (4.0 * math.pi),
+            scalar2=0.125,
+            op0=ALU.mult,
+            op1=ALU.add,
+        )
+        minus_thr = keep.tile([P, 1], F32, name="minus_thr")
+        nc.vector.tensor_scalar(
+            out=minus_thr[:], in0=spread[:, THR : THR + 1], scalar1=-1.0, scalar2=None, op0=ALU.mult
+        )
+        by_plane = turns[:].rearrange("p i w -> p w i")
+        pair_shape = [P, PLANES, LIMBS, LIMBS]
+        mid = keep.tile(pair_shape, F32, name="mid")
+        nc.vector.tensor_tensor(
+            out=mid[:],
+            in0=by_plane.unsqueeze(3).to_broadcast(pair_shape),
+            in1=by_plane.unsqueeze(2).to_broadcast(pair_shape),
+            op=ALU.add,
+        )
+        whole = keep.tile(pair_shape, F32, name="whole")
+        nc.vector.tensor_scalar(
+            out=whole[:], in0=mid[:], scalar1=ROUND_MAGIC, scalar2=ROUND_MAGIC, op0=ALU.add, op1=ALU.subtract
+        )
+        frac = keep.tile(pair_shape, F32, name="frac")
+        nc.vector.tensor_tensor(out=frac[:], in0=mid[:], in1=whole[:], op=ALU.subtract)
+
+        b_route_f = keep.tile([P, SLOTS], F32, name="b_route_f")
+        nc.gpsimd.tensor_copy(out=b_route_f[:], in_=b_route_bf[:].rearrange("q u e -> q (u e)"))
+        half_b_gate = keep.tile([P, SLOTS], F32, name="half_b_gate")
+        nc.gpsimd.tensor_scalar(
+            out=half_b_gate[:],
+            in0=b_gate_bf[:].rearrange("q u e -> q (u e)"),
+            scalar1=0.5,
+            scalar2=0.0,
+            op0=ALU.mult,
+            op1=ALU.add,
+        )
+
+        x_grouped = keep.tile([P, TOKENS, SLOTS], BF16, name="x_grouped", align_bytes=64)
+        x_codes = keep.tile([P, TOKENS], U32, name="x_codes", align_bytes=64)
+        x_scales = keep.tile([P, TOKENS], U8, name="x_scales", align_bytes=64)
+        wr_grouped = [keep.tile([P, HALF, SLOTS], BF16, name="wr_grouped%d" % u, align_bytes=64) for u in range(2)]
+        wr_codes = keep.tile([P, H], U32, name="wr_codes", align_bytes=64)
+        wr_scales = keep.tile([P, H], U8, name="wr_scales", align_bytes=64)
+
+        transpose_and_group(nc, psum, ident[:], [x_sb[:, n, :] for n in range(TOKEN_TILES)], x_grouped[:], True)
+        sin_cos = keep.tile([P, PLANES, LIMBS * LIMBS], F32, name="sin_cos")
+        nc.scalar.activation(
+            out=sin_cos[:].rearrange("p w n -> p (w n)"),
+            in_=frac[:].rearrange("p w i j -> p (w i j)"),
+            func=ACT.Sin,
+            scale=2.0 * math.pi,
+        )
+        for u in range(2):
+            transpose_and_group(
+                nc, psum, ident[:], [wr_sb[:, 2 * u + e, :] for e in range(2)], wr_grouped[u][:], u == 1
+            )
+        quantise(nc, x_grouped[:], x_codes[:], x_scales[:])
+        for u in range(2):
+            cols = slice(u * HALF, (u + 1) * HALF)
+            quantise(nc, wr_grouped[u][:], wr_codes[:, cols], wr_scales[:, cols])
+
+        b_route_t = psum.tile([P, SLOTS, P], F32, tag="bank", name="b_route_t")
+        for s in range(SLOTS):
+            nc.tensor.transpose(b_route_t[:, s, :], b_route_f[:, s : s + 1].to_broadcast([P, P]), ident[:])
+        b_route_rows = keep.tile([P, SLOTS, P], F32, name="b_route_rows")
+        nc.scalar.copy(out=b_route_rows[:], in_=b_route_t[:])
+
+        terms = keep.tile([P, COORDS, LIMBS * LIMBS], F32, name="terms")
+        nc.vector.tensor_tensor(out=terms[:, 0:2, :], in0=sin_cos[:, 0:2, :], in1=sin_cos[:, 4:6, :], op=ALU.mult)
+        nc.vector.tensor_tensor(out=terms[:, 2, :], in0=sin_cos[:, 2, :], in1=sin_cos[:, 3, :], op=ALU.mult)
+        gyroid = keep.tile([P, LIMBS, PAIRS], F32, name="gyroid")
+        nc.vector.tensor_reduce(
+            out=gyroid[:, :, 1:PAIRS],
+            in_=terms[:].rearrange("p c (i j) -> p i j c", j=LIMBS),
+            axis=AXIS_X,
+            op=ALU.add,
+        )
+        picked = keep.tile([P, LIMBS, LIMBS], F32, name="picked")
+        nc.vector.tensor_tensor(
+            out=picked[:],
+            in0=gyroid[:, :, 1:PAIRS],
+            in1=own_limb[:].unsqueeze(1).to_broadcast([P, LIMBS, LIMBS]),
+            op=ALU.mult,
+        )
+        nc.vector.tensor_reduce(out=gyroid[:, :, 0], in_=picked[:], axis=AXIS_X, op=ALU.add)
+        tanh_f = keep.tile([P, LIMBS, PAIRS], F32, name="tanh_f")
+        nc.scalar.activation(out=tanh_f[:], in_=gyroid[:], func=ACT.Tanh, bias=minus_thr[:, 0:1])
+
+        wg_parts = [(u, g) for u in range(2) for g in range(2)]
+        wg_grouped = {
+            part: keep.tile([P, HALF, SLOTS], BF16, name="wg_grouped%d%d" % part, align_bytes=64) for part in wg_parts
+        }
+        wg_codes = [keep.tile([P, H], U32, name="wg_codes%d" % g, align_bytes=64) for g in range(2)]
+        wg_scales = [keep.tile([P, H], U8, name="wg_scales%d" % g, align_bytes=64) for g in range(2)]
+
+        def group_w_gate(u, g):
+            rows = [wg_sb[:, 2 * u + e, g * H : (g + 1) * H] for e in range(2)]
+            transpose_and_group(nc, psum, ident[:], rows, wg_grouped[(u, g)][:], True)
+
+        group_w_gate(*wg_parts[0])
+
+        proj_ps = [psum.tile([P, BANK], F32, tag="bank", name="proj_ps%d" % n) for n in range(TOKEN_TILES)]
+        projected = [keep.tile([P, SLOTS, P], F32, name="projected%d" % n) for n in range(TOKEN_TILES)]
+        for n in range(TOKEN_TILES):
+            tokens = slice(n * P, (n + 1) * P)
+            for u in range(2):
+                cols = slice(u * HALF, (u + 1) * HALF)
+                nc.tensor.matmul_mx(
+                    out=proj_ps[n][:, cols],
+                    lhsT=x_codes[:, tokens].bitcast(FP8X4),
+                    lhsT_scale=x_scales[:, tokens],
+                    rhs=wr_codes[:, cols].bitcast(FP8X4),
+                    rhs_scale=wr_scales[:, cols],
+                    start=True,
+                    stop=True,
+                )
+
+        def add_b_route(n):
+            nc.vector.tensor_tensor(
+                out=projected[n][:].rearrange("t s q -> t (s q)"),
+                in0=proj_ps[n][:],
+                in1=b_route_rows[:].rearrange("t s q -> t (s q)"),
+                op=ALU.add,
+            )
+
+        add_b_route(0)
+
+        nc.vector.scalar_tensor_tensor(
+            out=twice_r[:, :, 0:PAIRS], in0=tanh_f[:], scalar=1.0, in1=two_on_diag, op0=ALU.add, op1=ALU.max
+        )
+        row_sum = keep.tile([P, LIMBS], F32, name="row_sum")
+        nc.vector.tensor_reduce(out=row_sum[:], in_=twice_r[:, :, 1 : PAIRS + 1], axis=AXIS_X, op=ALU.add)
+        row_inv = keep.tile([P, LIMBS], F32, name="row_inv")
+        nc.vector.reciprocal(out=row_inv[:], in_=row_sum[:])
+        to_limb = keep.tile([P, LIMBS], F32, name="to_limb")
+        nc.vector.tensor_tensor(out=to_limb[:], in0=twice_r[:, :, 0], in1=row_inv[:], op=ALU.mult)
+        mixer = keep.tile([P, GROUPS, LIMBS], F32, name="mixer")
+        nc.vector.tensor_tensor(
+            out=mixer[:],
+            in0=own_group[:].unsqueeze(2).to_broadcast([P, GROUPS, LIMBS]),
+            in1=to_limb[:].unsqueeze(1).to_broadcast([P, GROUPS, LIMBS]),
+            op=ALU.mult,
+        )
+
+        add_b_route(1)
+
+        for part in wg_parts[1:]:
+            group_w_gate(*part)
+        for u, g in wg_parts:
+            cols = slice(u * HALF, (u + 1) * HALF)
+            quantise(nc, wg_grouped[(u, g)][:], wg_codes[g][:, cols], wg_scales[g][:, cols])
+
+        r_codes = keep.tile([P, TOKENS], U32, name="r_codes", align_bytes=64)
+        r_scales = keep.tile([P, TOKENS], U8, name="r_scales", align_bytes=64)
+        diff = [keep.tile([P, SLOTS, P], F32, name="diff%d" % n) for n in range(TOKEN_TILES)]
+        for n in range(TOKEN_TILES):
+            tokens = slice(n * P, (n + 1) * P)
+            routed_ps = psum.tile([P, SLOTS, P], F32, tag="bank", name="routed_ps")
+            for s in range(SLOTS):
+                nc.tensor.matmul(
+                    out=routed_ps[:, s, :],
+                    lhsT=projected[n][:, s, :],
+                    rhs=mixer[:].rearrange("t a i -> t (a i)"),
+                    start=True,
+                    stop=True,
+                )
+            r_grouped = keep.tile([P, P, SLOTS], BF16, name="r_grouped%d" % n, align_bytes=64)
+            nc.scalar.copy(out=r_grouped[:], in_=routed_ps[:].rearrange("q s t -> q t s"))
+            quantise(nc, r_grouped[:], r_codes[:, tokens], r_scales[:, tokens])
+            nc.vector.tensor_tensor(
+                out=diff[n][:],
+                in0=routed_ps[:],
+                in1=x_grouped[:, tokens, :].rearrange("q t s -> q s t"),
+                op=ALU.subtract,
+            )
+
+        units = [(n, u) for n in range(TOKEN_TILES) for u in range(2)]
+        tanh_g = {unit: keep.tile([P, 2, P], F32, name="tanh_g%d%d" % unit) for unit in units}
+        for n, u in units:
+            tokens = slice(n * P, (n + 1) * P)
+            gate_ps = psum.tile([P, 2, P], F32, tag="bank", name="gate_ps")
+            for e in range(2):
+                feats = slice((2 * u + e) * P, (2 * u + e + 1) * P)
+                for g, (codes, scales) in enumerate(((x_codes, x_scales), (r_codes, r_scales))):
+                    nc.tensor.matmul_mx(
+                        out=gate_ps[:, e, :],
+                        lhsT=wg_codes[g][:, feats].bitcast(FP8X4),
+                        lhsT_scale=wg_scales[g][:, feats],
+                        rhs=codes[:, tokens].bitcast(FP8X4),
+                        rhs_scale=scales[:, tokens],
+                        start=(g == 0),
+                        stop=(g == 1),
+                    )
+            for e in range(2):
+                nc.scalar.activation(
+                    out=tanh_g[(n, u)][:, e, :],
+                    in_=gate_ps[:, e, :],
+                    func=ACT.Tanh,
+                    scale=0.5,
+                    bias=half_b_gate[:, 2 * u + e : 2 * u + e + 1],
+                )
+
+        moved_t = {}
+
+        def weigh_and_transpose(n, u):
+            moved = keep.tile([P, 2, P], F32, name="moved%d%d" % (n, u))
+            nc.vector.scalar_tensor_tensor(
+                out=moved[:].rearrange("q e t -> q (e t)"),
+                in0=tanh_g[(n, u)][:].rearrange("q e t -> q (e t)"),
+                scalar=1.0,
+                in1=diff[n][:, 2 * u : 2 * u + 2, :].rearrange("q e t -> q (e t)"),
+                op0=ALU.add,
+                op1=ALU.mult,
+            )
+            moved_t[(n, u)] = psum.tile([P, 2, P], F32, tag="bank", name="moved_t")
+            for e in range(2):
+                nc.tensor.transpose(moved_t[(n, u)][:, e, :], moved[:, e, :], ident[:])
+
+        def add_x_and_store(n, u):
+            feats = slice(u * HALF, (u + 1) * HALF)
+            out_sb = keep.tile([P, HALF], F32, name="out_sb%d%d" % (n, u))
+            nc.vector.scalar_tensor_tensor(
+                out=out_sb[:].rearrange("t (q e) -> t q e", e=2),
+                in0=moved_t[(n, u)][:].rearrange("t e q -> t q e"),
+                scalar=0.5,
+                in1=x_sb[:, n, feats].rearrange("t (q e) -> t q e", e=2),
+                op0=ALU.mult,
+                op1=ALU.add,
+            )
+            nc.sync.dma_start(out=out_rows[n * P : (n + 1) * P, feats], in_=out_sb[:])
+
+        weigh_and_transpose(*units[0])
+        for k in range(1, len(units)):
+            weigh_and_transpose(*units[k])
+            add_x_and_store(*units[k - 1])
+        add_x_and_store(*units[-1])

@@ -55,22 +55,21 @@ def tile_tpmslimbrouter_pa_s_kernel(
     with ExitStack() as ctx:
         keep = ctx.enter_context(tc.tile_pool(name="keep", bufs=1))
         psum = ctx.enter_context(tc.psum_pool(name="psum", bufs=8))
-        ctx.enter_context(tc.manual_schedule())
 
-        ident = keep.tile([P, P], F32, name="ident")
-        make_identity(nc, ident[:])
+        smalls = keep.tile([P, 64], BF16, name="smalls")
+        nc.gpsimd.memset(smalls[:], 0.0)
         ones = keep.tile([P, P], BF16, name="ones")
         nc.gpsimd.memset(ones[:], 1.0)
-        smalls = keep.tile([P, 64], BF16, name="smalls")
-        nc.vector.memset(smalls[:], 0.0)
+        ident = keep.tile([P, P], F32, name="ident")
+        make_identity(nc, ident[:])
         warm = keep.tile([P, 1], F32, name="warm")
         nc.vector.memset(warm[:], 0.0)
 
         THR = 32
-        nc.scalar.dma_start(
+        nc.sync.dma_start(
             out=smalls[0:1, 0 : LIMBS * COORDS], in_=limb_positions.rearrange("i c -> (i c)").unsqueeze(0)
         )
-        nc.scalar.dma_start(out=smalls[0:1, THR : THR + 1], in_=channel_threshold.unsqueeze(0))
+        nc.sync.dma_start(out=smalls[0:1, THR : THR + 1], in_=channel_threshold.unsqueeze(0))
         b_route_bf = keep.tile([P, 2, 2], BF16, name="b_route_bf")
         nc.scalar.dma_start(out=b_route_bf[:], in_=b_route.rearrange("(u q e) -> q u e", u=2, e=2))
         b_gate_bf = keep.tile([P, 2, 2], BF16, name="b_gate_bf")

@@ -55,21 +55,20 @@ def tile_tpmslimbrouter_pa_s_kernel(
     with ExitStack() as ctx:
         keep = ctx.enter_context(tc.tile_pool(name="keep", bufs=1))
         psum = ctx.enter_context(tc.psum_pool(name="psum", bufs=8))
+        ctx.enter_context(tc.manual_schedule())
 
-        smalls = keep.tile([P, 64], BF16, name="smalls")
-        nc.gpsimd.memset(smalls[:], 0.0)
-        ones = keep.tile([P, P], BF16, name="ones")
-        nc.gpsimd.memset(ones[:], 1.0)
+        small_col = keep.tile([P, 1], BF16, name="small_col")
+        nc.gpsimd.memset(small_col[:], 0.0)
         ident = keep.tile([P, P], F32, name="ident")
         make_identity(nc, ident[:])
         warm = keep.tile([P, 1], F32, name="warm")
         nc.vector.memset(warm[:], 0.0)
 
-        THR = 32
-        nc.sync.dma_start(
-            out=smalls[0:1, 0 : LIMBS * COORDS], in_=limb_positions.rearrange("i c -> (i c)").unsqueeze(0)
-        )
-        nc.sync.dma_start(out=smalls[0:1, THR : THR + 1], in_=channel_threshold.unsqueeze(0))
+        N_POS = LIMBS * COORDS
+        pos_flat = limb_positions.rearrange("i c -> (i c)").unsqueeze(1)
+        nc.sync.dma_start(out=small_col[0:16, :], in_=pos_flat[0:16, :])
+        nc.sync.dma_start(out=small_col[16:N_POS, :], in_=pos_flat[16:N_POS, :])
+        nc.sync.dma_start(out=small_col[N_POS : N_POS + 1, :], in_=channel_threshold.unsqueeze(1))
         b_route_bf = keep.tile([P, 2, 2], BF16, name="b_route_bf")
         nc.scalar.dma_start(out=b_route_bf[:], in_=b_route.rearrange("(u q e) -> q u e", u=2, e=2))
         b_gate_bf = keep.tile([P, 2, 2], BF16, name="b_gate_bf")
@@ -105,33 +104,38 @@ def tile_tpmslimbrouter_pa_s_kernel(
         twice_r = keep.tile([P, LIMBS, PAIRS + 1], F32, name="twice_r")
         nc.vector.memset(twice_r[:, :, PAIRS], 2.0e-6)
 
-        spread = psum.tile([P, BANK], F32, tag="bank", name="spread")
-        nc.tensor.matmul(out=spread[:, 0:64], lhsT=ones[:], rhs=smalls[:], start=True, stop=True)
         PLANES = 2 * COORDS
-        positions = spread[:, 0 : LIMBS * COORDS].rearrange("p (i c) -> p i c", c=COORDS)
-        turns = keep.tile([P, LIMBS, PLANES], F32, name="turns")
-        nc.vector.tensor_scalar(
-            out=turns[:, :, 0:COORDS], in0=positions, scalar1=1.0 / (4.0 * math.pi), scalar2=None, op0=ALU.mult
+        THR = PLANES * LIMBS
+        comb = keep.tile([P, 64], BF16, name="comb")
+        nc.vector.memset(comb[:], 0.0)
+        unit = ident[:, 0:N_POS].rearrange("k (i c) -> k c i", c=COORDS)
+        planes = comb[:, 0:THR].rearrange("k (g c i) -> k g c i", g=2, c=COORDS)
+        for g, op in enumerate((ALU.add, ALU.subtract)):
+            nc.vector.tensor_tensor(out=planes[:, g, 0:2, :], in0=unit[:, 0:2, :], in1=unit[:, 1:3, :], op=op)
+            nc.vector.tensor_tensor(out=planes[:, g, 2, :], in0=unit[:, 2, :], in1=unit[:, 0, :], op=op)
+        nc.vector.tensor_copy(out=comb[:, THR : THR + 1], in_=ident[:, N_POS : N_POS + 1])
+        combos = psum.tile([P, BANK], F32, tag="bank", name="combos")
+        nc.tensor.matmul(
+            out=combos[:, 0:64], lhsT=small_col[:, 0:1].to_broadcast([P, P]), rhs=comb[:], start=True, stop=True
         )
+        turns = keep.tile([P, PLANES, LIMBS], F32, name="turns")
         nc.vector.tensor_scalar(
-            out=turns[:, :, COORDS:PLANES],
-            in0=positions,
+            out=turns[:].rearrange("p w i -> p (w i)"),
+            in0=combos[:, 0:THR],
             scalar1=1.0 / (4.0 * math.pi),
-            scalar2=0.125,
+            scalar2=None,
             op0=ALU.mult,
-            op1=ALU.add,
         )
         minus_thr = keep.tile([P, 1], F32, name="minus_thr")
         nc.vector.tensor_scalar(
-            out=minus_thr[:], in0=spread[:, THR : THR + 1], scalar1=-1.0, scalar2=None, op0=ALU.mult
+            out=minus_thr[:], in0=combos[:, THR : THR + 1], scalar1=-1.0, scalar2=None, op0=ALU.mult
         )
-        by_plane = turns[:].rearrange("p i w -> p w i")
         pair_shape = [P, PLANES, LIMBS, LIMBS]
         mid = keep.tile(pair_shape, F32, name="mid")
         nc.vector.tensor_tensor(
             out=mid[:],
-            in0=by_plane.unsqueeze(3).to_broadcast(pair_shape),
-            in1=by_plane.unsqueeze(2).to_broadcast(pair_shape),
+            in0=turns[:].unsqueeze(3).to_broadcast(pair_shape),
+            in1=turns[:].unsqueeze(2).to_broadcast(pair_shape),
             op=ALU.add,
         )
         whole = keep.tile(pair_shape, F32, name="whole")
@@ -161,35 +165,20 @@ def tile_tpmslimbrouter_pa_s_kernel(
         wr_scales = keep.tile([P, H], U8, name="wr_scales", align_bytes=64)
 
         transpose_and_group(nc, psum, ident[:], [x_sb[:, n, :] for n in range(TOKEN_TILES)], x_grouped[:], True)
-        sin_cos = keep.tile([P, PLANES, LIMBS * LIMBS], F32, name="sin_cos")
+        sines = keep.tile([P, PLANES, LIMBS * LIMBS], F32, name="sines")
         nc.scalar.activation(
-            out=sin_cos[:].rearrange("p w n -> p (w n)"),
+            out=sines[:].rearrange("p w n -> p (w n)"),
             in_=frac[:].rearrange("p w i j -> p (w i j)"),
             func=ACT.Sin,
             scale=2.0 * math.pi,
         )
         for u in range(2):
-            transpose_and_group(
-                nc, psum, ident[:], [wr_sb[:, 2 * u + e, :] for e in range(2)], wr_grouped[u][:], u == 1
-            )
+            transpose_and_group(nc, psum, ident[:], [wr_sb[:, 2 * u + e, :] for e in range(2)], wr_grouped[u][:], True)
         quantise(nc, x_grouped[:], x_codes[:], x_scales[:])
-        for u in range(2):
-            cols = slice(u * HALF, (u + 1) * HALF)
-            quantise(nc, wr_grouped[u][:], wr_codes[:, cols], wr_scales[:, cols])
-
-        b_route_t = psum.tile([P, SLOTS, P], F32, tag="bank", name="b_route_t")
-        for s in range(SLOTS):
-            nc.tensor.transpose(b_route_t[:, s, :], b_route_f[:, s : s + 1].to_broadcast([P, P]), ident[:])
-        b_route_rows = keep.tile([P, SLOTS, P], F32, name="b_route_rows")
-        nc.scalar.copy(out=b_route_rows[:], in_=b_route_t[:])
-
-        terms = keep.tile([P, COORDS, LIMBS * LIMBS], F32, name="terms")
-        nc.vector.tensor_tensor(out=terms[:, 0:2, :], in0=sin_cos[:, 0:2, :], in1=sin_cos[:, 4:6, :], op=ALU.mult)
-        nc.vector.tensor_tensor(out=terms[:, 2, :], in0=sin_cos[:, 2, :], in1=sin_cos[:, 3, :], op=ALU.mult)
         gyroid = keep.tile([P, LIMBS, PAIRS], F32, name="gyroid")
         nc.vector.tensor_reduce(
             out=gyroid[:, :, 1:PAIRS],
-            in_=terms[:].rearrange("p c (i j) -> p i j c", j=LIMBS),
+            in_=sines[:].rearrange("p w (i j) -> p i j w", j=LIMBS),
             axis=AXIS_X,
             op=ALU.add,
         )
@@ -202,7 +191,17 @@ def tile_tpmslimbrouter_pa_s_kernel(
         )
         nc.vector.tensor_reduce(out=gyroid[:, :, 0], in_=picked[:], axis=AXIS_X, op=ALU.add)
         tanh_f = keep.tile([P, LIMBS, PAIRS], F32, name="tanh_f")
-        nc.scalar.activation(out=tanh_f[:], in_=gyroid[:], func=ACT.Tanh, bias=minus_thr[:, 0:1])
+        nc.scalar.activation(out=tanh_f[:], in_=gyroid[:], func=ACT.Tanh, scale=0.5, bias=minus_thr[:, 0:1])
+
+        b_route_t = psum.tile([P, SLOTS, P], F32, tag="bank", name="b_route_t")
+        for s in range(SLOTS):
+            nc.tensor.transpose(b_route_t[:, s, :], b_route_f[:, s : s + 1].to_broadcast([P, P]), ident[:])
+        b_route_rows = keep.tile([P, SLOTS, P], F32, name="b_route_rows")
+        nc.scalar.copy(out=b_route_rows[:], in_=b_route_t[:])
+
+        for u in range(2):
+            cols = slice(u * HALF, (u + 1) * HALF)
+            quantise(nc, wr_grouped[u][:], wr_codes[:, cols], wr_scales[:, cols])
 
         wg_parts = [(u, g) for u in range(2) for g in range(2)]
         wg_grouped = {
@@ -215,7 +214,25 @@ def tile_tpmslimbrouter_pa_s_kernel(
             rows = [wg_sb[:, 2 * u + e, g * H : (g + 1) * H] for e in range(2)]
             transpose_and_group(nc, psum, ident[:], rows, wg_grouped[(u, g)][:], True)
 
-        group_w_gate(*wg_parts[0])
+        for part in wg_parts[0:2]:
+            group_w_gate(*part)
+
+        nc.vector.scalar_tensor_tensor(
+            out=twice_r[:, :, 0:PAIRS], in0=tanh_f[:], scalar=1.0, in1=two_on_diag, op0=ALU.add, op1=ALU.max
+        )
+        row_sum = keep.tile([P, LIMBS], F32, name="row_sum")
+        nc.vector.tensor_reduce(out=row_sum[:], in_=twice_r[:, :, 1 : PAIRS + 1], axis=AXIS_X, op=ALU.add)
+        row_inv = keep.tile([P, LIMBS], F32, name="row_inv")
+        nc.vector.reciprocal(out=row_inv[:], in_=row_sum[:])
+        to_limb = keep.tile([P, LIMBS], F32, name="to_limb")
+        nc.vector.tensor_tensor(out=to_limb[:], in0=twice_r[:, :, 0], in1=row_inv[:], op=ALU.mult)
+        mixer = keep.tile([P, GROUPS, LIMBS], F32, name="mixer")
+        nc.vector.tensor_tensor(
+            out=mixer[:],
+            in0=own_group[:].unsqueeze(2).to_broadcast([P, GROUPS, LIMBS]),
+            in1=to_limb[:].unsqueeze(1).to_broadcast([P, GROUPS, LIMBS]),
+            op=ALU.mult,
+        )
 
         proj_ps = [psum.tile([P, BANK], F32, tag="bank", name="proj_ps%d" % n) for n in range(TOKEN_TILES)]
         projected = [keep.tile([P, SLOTS, P], F32, name="projected%d" % n) for n in range(TOKEN_TILES)]
@@ -242,27 +259,9 @@ def tile_tpmslimbrouter_pa_s_kernel(
             )
 
         add_b_route(0)
-
-        nc.vector.scalar_tensor_tensor(
-            out=twice_r[:, :, 0:PAIRS], in0=tanh_f[:], scalar=1.0, in1=two_on_diag, op0=ALU.add, op1=ALU.max
-        )
-        row_sum = keep.tile([P, LIMBS], F32, name="row_sum")
-        nc.vector.tensor_reduce(out=row_sum[:], in_=twice_r[:, :, 1 : PAIRS + 1], axis=AXIS_X, op=ALU.add)
-        row_inv = keep.tile([P, LIMBS], F32, name="row_inv")
-        nc.vector.reciprocal(out=row_inv[:], in_=row_sum[:])
-        to_limb = keep.tile([P, LIMBS], F32, name="to_limb")
-        nc.vector.tensor_tensor(out=to_limb[:], in0=twice_r[:, :, 0], in1=row_inv[:], op=ALU.mult)
-        mixer = keep.tile([P, GROUPS, LIMBS], F32, name="mixer")
-        nc.vector.tensor_tensor(
-            out=mixer[:],
-            in0=own_group[:].unsqueeze(2).to_broadcast([P, GROUPS, LIMBS]),
-            in1=to_limb[:].unsqueeze(1).to_broadcast([P, GROUPS, LIMBS]),
-            op=ALU.mult,
-        )
-
         add_b_route(1)
 
-        for part in wg_parts[1:]:
+        for part in wg_parts[2:4]:
             group_w_gate(*part)
         for u, g in wg_parts:
             cols = slice(u * HALF, (u + 1) * HALF)
@@ -347,8 +346,7 @@ def tile_tpmslimbrouter_pa_s_kernel(
             )
             nc.sync.dma_start(out=out_rows[n * P : (n + 1) * P, feats], in_=out_sb[:])
 
-        weigh_and_transpose(*units[0])
-        for k in range(1, len(units)):
-            weigh_and_transpose(*units[k])
-            add_x_and_store(*units[k - 1])
-        add_x_and_store(*units[-1])
+        for unit in units:
+            weigh_and_transpose(*unit)
+        for unit in units:
+            add_x_and_store(*unit)

@@ -164,7 +164,7 @@ def tile_tpmslimbrouter_pa_s_kernel(
         wr_codes = keep.tile([P, H], U32, name="wr_codes", align_bytes=64)
         wr_scales = keep.tile([P, H], U8, name="wr_scales", align_bytes=64)
 
-        transpose_and_group(nc, psum, ident[:], [x_sb[:, n, :] for n in range(TOKEN_TILES)], x_grouped[:], True)
+        transpose_and_group(nc, psum, ident[:], [x_sb[:, n, :] for n in range(TOKEN_TILES)], x_grouped[:], False)
         sines = keep.tile([P, PLANES, LIMBS * LIMBS], F32, name="sines")
         nc.scalar.activation(
             out=sines[:].rearrange("p w n -> p (w n)"),
@@ -174,24 +174,6 @@ def tile_tpmslimbrouter_pa_s_kernel(
         )
         for u in range(2):
             transpose_and_group(nc, psum, ident[:], [wr_sb[:, 2 * u + e, :] for e in range(2)], wr_grouped[u][:], True)
-        quantise(nc, x_grouped[:], x_codes[:], x_scales[:])
-        gyroid = keep.tile([P, LIMBS, PAIRS], F32, name="gyroid")
-        nc.vector.tensor_reduce(
-            out=gyroid[:, :, 1:PAIRS],
-            in_=sines[:].rearrange("p w (i j) -> p i j w", j=LIMBS),
-            axis=AXIS_X,
-            op=ALU.add,
-        )
-        picked = keep.tile([P, LIMBS, LIMBS], F32, name="picked")
-        nc.vector.tensor_tensor(
-            out=picked[:],
-            in0=gyroid[:, :, 1:PAIRS],
-            in1=own_limb[:].unsqueeze(1).to_broadcast([P, LIMBS, LIMBS]),
-            op=ALU.mult,
-        )
-        nc.vector.tensor_reduce(out=gyroid[:, :, 0], in_=picked[:], axis=AXIS_X, op=ALU.add)
-        tanh_f = keep.tile([P, LIMBS, PAIRS], F32, name="tanh_f")
-        nc.scalar.activation(out=tanh_f[:], in_=gyroid[:], func=ACT.Tanh, scale=0.5, bias=minus_thr[:, 0:1])
 
         b_route_t = psum.tile([P, SLOTS, P], F32, tag="bank", name="b_route_t")
         for s in range(SLOTS):
@@ -199,9 +181,26 @@ def tile_tpmslimbrouter_pa_s_kernel(
         b_route_rows = keep.tile([P, SLOTS, P], F32, name="b_route_rows")
         nc.scalar.copy(out=b_route_rows[:], in_=b_route_t[:])
 
-        for u in range(2):
-            cols = slice(u * HALF, (u + 1) * HALF)
-            quantise(nc, wr_grouped[u][:], wr_codes[:, cols], wr_scales[:, cols])
+        gyroid = keep.tile([P, LIMBS, PAIRS], F32, name="gyroid")
+        nc.vector.tensor_reduce(
+            out=gyroid[:, :, 1:PAIRS],
+            in_=sines[:].rearrange("p w (i j) -> p i j w", j=LIMBS),
+            axis=AXIS_X,
+            op=ALU.add,
+        )
+        quantise(nc, x_grouped[:], x_codes[:], x_scales[:])
+        picked = keep.tile([P, LIMBS, LIMBS], F32, name="picked")
+        nc.vector.tensor_tensor(
+            out=picked[:],
+            in0=gyroid[:, :, 1:PAIRS],
+            in1=own_limb[:].unsqueeze(1).to_broadcast([P, LIMBS, LIMBS]),
+            op=ALU.mult,
+        )
+        quantise(nc, wr_grouped[0][:], wr_codes[:, 0:HALF], wr_scales[:, 0:HALF])
+        nc.vector.tensor_reduce(out=gyroid[:, :, 0], in_=picked[:], axis=AXIS_X, op=ALU.add)
+        tanh_f = keep.tile([P, LIMBS, PAIRS], F32, name="tanh_f")
+        nc.scalar.activation(out=tanh_f[:], in_=gyroid[:], func=ACT.Tanh, scale=0.5, bias=minus_thr[:, 0:1])
+        quantise(nc, wr_grouped[1][:], wr_codes[:, HALF:H], wr_scales[:, HALF:H])
 
         wg_parts = [(u, g) for u in range(2) for g in range(2)]
         wg_grouped = {
@@ -216,23 +215,6 @@ def tile_tpmslimbrouter_pa_s_kernel(
 
         for part in wg_parts[0:2]:
             group_w_gate(*part)
-
-        nc.vector.scalar_tensor_tensor(
-            out=twice_r[:, :, 0:PAIRS], in0=tanh_f[:], scalar=1.0, in1=two_on_diag, op0=ALU.add, op1=ALU.max
-        )
-        row_sum = keep.tile([P, LIMBS], F32, name="row_sum")
-        nc.vector.tensor_reduce(out=row_sum[:], in_=twice_r[:, :, 1 : PAIRS + 1], axis=AXIS_X, op=ALU.add)
-        row_inv = keep.tile([P, LIMBS], F32, name="row_inv")
-        nc.vector.reciprocal(out=row_inv[:], in_=row_sum[:])
-        to_limb = keep.tile([P, LIMBS], F32, name="to_limb")
-        nc.vector.tensor_tensor(out=to_limb[:], in0=twice_r[:, :, 0], in1=row_inv[:], op=ALU.mult)
-        mixer = keep.tile([P, GROUPS, LIMBS], F32, name="mixer")
-        nc.vector.tensor_tensor(
-            out=mixer[:],
-            in0=own_group[:].unsqueeze(2).to_broadcast([P, GROUPS, LIMBS]),
-            in1=to_limb[:].unsqueeze(1).to_broadcast([P, GROUPS, LIMBS]),
-            op=ALU.mult,
-        )
 
         proj_ps = [psum.tile([P, BANK], F32, tag="bank", name="proj_ps%d" % n) for n in range(TOKEN_TILES)]
         projected = [keep.tile([P, SLOTS, P], F32, name="projected%d" % n) for n in range(TOKEN_TILES)]
@@ -250,16 +232,35 @@ def tile_tpmslimbrouter_pa_s_kernel(
                     stop=True,
                 )
 
-        def add_b_route(n):
+        def add_b_route(n, u):
+            cols = slice(u * HALF, (u + 1) * HALF)
             nc.vector.tensor_tensor(
-                out=projected[n][:].rearrange("t s q -> t (s q)"),
-                in0=proj_ps[n][:],
-                in1=b_route_rows[:].rearrange("t s q -> t (s q)"),
+                out=projected[n][:].rearrange("t s q -> t (s q)")[:, cols],
+                in0=proj_ps[n][:, cols],
+                in1=b_route_rows[:].rearrange("t s q -> t (s q)")[:, cols],
                 op=ALU.add,
             )
 
-        add_b_route(0)
-        add_b_route(1)
+        nc.vector.scalar_tensor_tensor(
+            out=twice_r[:, :, 0:PAIRS], in0=tanh_f[:], scalar=1.0, in1=two_on_diag, op0=ALU.add, op1=ALU.max
+        )
+        add_b_route(0, 0)
+        row_sum = keep.tile([P, LIMBS], F32, name="row_sum")
+        nc.vector.tensor_reduce(out=row_sum[:], in_=twice_r[:, :, 1 : PAIRS + 1], axis=AXIS_X, op=ALU.add)
+        add_b_route(0, 1)
+        row_inv = keep.tile([P, LIMBS], F32, name="row_inv")
+        nc.vector.reciprocal(out=row_inv[:], in_=row_sum[:])
+        to_limb = keep.tile([P, LIMBS], F32, name="to_limb")
+        nc.vector.tensor_tensor(out=to_limb[:], in0=twice_r[:, :, 0], in1=row_inv[:], op=ALU.mult)
+        mixer = keep.tile([P, GROUPS, LIMBS], F32, name="mixer")
+        nc.vector.tensor_tensor(
+            out=mixer[:],
+            in0=own_group[:].unsqueeze(2).to_broadcast([P, GROUPS, LIMBS]),
+            in1=to_limb[:].unsqueeze(1).to_broadcast([P, GROUPS, LIMBS]),
+            op=ALU.mult,
+        )
+        for u in range(2):
+            add_b_route(1, u)
 
         for part in wg_parts[2:4]:
             group_w_gate(*part)

@@ -66,9 +66,9 @@ def tile_tpmslimbrouter_pa_s_kernel(
 
         N_POS = LIMBS * COORDS
         pos_flat = limb_positions.rearrange("i c -> (i c)").unsqueeze(1)
-        nc.sync.dma_start(out=small_col[0:16, :], in_=pos_flat[0:16, :])
-        nc.sync.dma_start(out=small_col[16:N_POS, :], in_=pos_flat[16:N_POS, :])
-        nc.sync.dma_start(out=small_col[N_POS : N_POS + 1, :], in_=channel_threshold.unsqueeze(1))
+        nc.scalar.dma_start(out=small_col[0:16, :], in_=pos_flat[0:16, :])
+        nc.scalar.dma_start(out=small_col[16:N_POS, :], in_=pos_flat[16:N_POS, :])
+        nc.scalar.dma_start(out=small_col[N_POS : N_POS + 1, :], in_=channel_threshold.unsqueeze(1))
         b_route_bf = keep.tile([P, 2, 2], BF16, name="b_route_bf")
         nc.scalar.dma_start(out=b_route_bf[:], in_=b_route.rearrange("(u q e) -> q u e", u=2, e=2))
         b_gate_bf = keep.tile([P, 2, 2], BF16, name="b_gate_bf")
@@ -292,16 +292,15 @@ def tile_tpmslimbrouter_pa_s_kernel(
                 op=ALU.subtract,
             )
 
-        units = [(n, u) for n in range(TOKEN_TILES) for u in range(2)]
-        tanh_g = {unit: keep.tile([P, 2, P], F32, name="tanh_g%d%d" % unit) for unit in units}
-        for n, u in units:
+        tanh_g = [keep.tile([P, SLOTS, P], F32, name="tanh_g%d" % n) for n in range(TOKEN_TILES)]
+        for n in range(TOKEN_TILES):
             tokens = slice(n * P, (n + 1) * P)
-            gate_ps = psum.tile([P, 2, P], F32, tag="bank", name="gate_ps")
-            for e in range(2):
-                feats = slice((2 * u + e) * P, (2 * u + e + 1) * P)
-                for g, (codes, scales) in enumerate(((x_codes, x_scales), (r_codes, r_scales))):
+            gate_ps = [psum.tile([P, P], F32, tag="bank", name="gate_ps%d" % s) for s in range(SLOTS)]
+            for g, (codes, scales) in enumerate(((x_codes, x_scales), (r_codes, r_scales))):
+                for s in range(SLOTS):
+                    feats = slice(s * P, (s + 1) * P)
                     nc.tensor.matmul_mx(
-                        out=gate_ps[:, e, :],
+                        out=gate_ps[s][:],
                         lhsT=wg_codes[g][:, feats].bitcast(FP8X4),
                         lhsT_scale=wg_scales[g][:, feats],
                         rhs=codes[:, tokens].bitcast(FP8X4),
@@ -309,22 +308,23 @@ def tile_tpmslimbrouter_pa_s_kernel(
                         start=(g == 0),
                         stop=(g == 1),
                     )
-            for e in range(2):
+            for s in range(SLOTS):
                 nc.scalar.activation(
-                    out=tanh_g[(n, u)][:, e, :],
-                    in_=gate_ps[:, e, :],
+                    out=tanh_g[n][:, s, :],
+                    in_=gate_ps[s][:],
                     func=ACT.Tanh,
                     scale=0.5,
-                    bias=half_b_gate[:, 2 * u + e : 2 * u + e + 1],
+                    bias=half_b_gate[:, s : s + 1],
                 )
 
+        units = [(n, u) for n in range(TOKEN_TILES) for u in range(2)]
         moved_t = {}
 
         def weigh_and_transpose(n, u):
             moved = keep.tile([P, 2, P], F32, name="moved%d%d" % (n, u))
             nc.vector.scalar_tensor_tensor(
                 out=moved[:].rearrange("q e t -> q (e t)"),
-                in0=tanh_g[(n, u)][:].rearrange("q e t -> q (e t)"),
+                in0=tanh_g[n][:, 2 * u : 2 * u + 2, :].rearrange("q e t -> q (e t)"),
                 scalar=1.0,
                 in1=diff[n][:, 2 * u : 2 * u + 2, :].rearrange("q e t -> q (e t)"),
                 op0=ALU.add,

import math
from contextlib import ExitStack

import concourse.mybir as mybir
from concourse.masks import make_identity

F32 = mybir.dt.float32
BF16 = mybir.dt.bfloat16
U32 = mybir.dt.uint32
U8 = mybir.dt.uint8
FP8X4 = mybir.dt.float8_e4m3fn_x4
ALU = mybir.AluOpType
ACT = mybir.ActivationFunctionType
AXIS_X = mybir.AxisListType.X

P = 128
TOKENS = 256
TOKEN_TILES = TOKENS // P
LIMBS = 8
GROUPS = P // LIMBS
COORDS = 3
H = 512
SLOTS = 4
BANK = 512
HALF = BANK // 2
ROUND_MAGIC = 1.5 * 2.0**23

FLOPS = 2 * TOKENS * H * H + 2 * TOKENS * 2 * H * H + 2 * TOKENS * LIMBS * H


def transpose_and_group(nc, psum, ident, row_blocks, grouped, on_scalar):
    bank = psum.tile([P, 2, HALF], F32, tag="bank", name="words_t")
    for b, rows in enumerate(row_blocks):
        words = rows.bitcast(F32)
        for u in range(2):
            nc.tensor.transpose(bank[:, u, b * P : (b + 1) * P], words[:, u * P : (u + 1) * P], ident)
    interleaved = bank[:].rearrange("q u c -> q c u")
    if on_scalar:
        nc.scalar.copy(out=grouped.bitcast(F32), in_=interleaved)
    else:
        nc.vector.tensor_copy(out=grouped.bitcast(F32), in_=interleaved)


def quantise(nc, grouped, codes, scales):
    nc.vector.quantize_mx(out=codes.bitcast(FP8X4), scales=scales, in_=grouped.rearrange("q c s -> q (c s)"))


def tile_tpmslimbrouter_pa_s_kernel(
    tc, x, limb_positions, channel_threshold, W_route, b_route, W_gate, b_gate, out
):
    nc = tc.nc
    x_rows = x.flatten_outer_dims()
    out_rows = out.flatten_outer_dims()

    with ExitStack() as ctx:
        keep = ctx.enter_context(tc.tile_pool(name="keep", bufs=1))
        psum = ctx.enter_context(tc.psum_pool(name="psum", bufs=8))
        ctx.enter_context(tc.manual_schedule())

        small_col = keep.tile([P, 1], BF16, name="small_col")
        nc.gpsimd.memset(small_col[:], 0.0)
        ident = keep.tile([P, P], F32, name="ident")
        make_identity(nc, ident[:])
        warm = keep.tile([P, 1], F32, name="warm")
        nc.vector.memset(warm[:], 0.0)

        N_POS = LIMBS * COORDS
        pos_flat = limb_positions.rearrange("i c -> (i c)").unsqueeze(1)
        nc.scalar.dma_start(out=small_col[0:16, :], in_=pos_flat[0:16, :])
        nc.scalar.dma_start(out=small_col[16:N_POS, :], in_=pos_flat[16:N_POS, :])
        nc.scalar.dma_start(out=small_col[N_POS : N_POS + 1, :], in_=channel_threshold.unsqueeze(1))
        b_route_bf = keep.tile([P, 2, 2], BF16, name="b_route_bf")
        nc.scalar.dma_start(out=b_route_bf[:], in_=b_route.rearrange("(u q e) -> q u e", u=2, e=2))
        b_gate_bf = keep.tile([P, 2, 2], BF16, name="b_gate_bf")
        nc.scalar.dma_start(out=b_gate_bf[:], in_=b_gate.rearrange("(u q e) -> q u e", u=2, e=2))

        x_sb = keep.tile([P, TOKEN_TILES, H], BF16, name="x_sb")
        nc.sync.dma_start(out=x_sb[:], in_=x_rows.rearrange("(n p) k -> p n k", p=P))
        wr_sb = keep.tile([P, SLOTS, H], BF16, name="wr_sb")
        wg_sb = keep.tile([P, SLOTS, 2 * H], BF16, name="wg_sb")
        for w_sb, w in ((wr_sb, W_route), (wg_sb, W_gate)):
            for u in range(2):
                nc.sync.dma_start(
                    out=w_sb[:, 2 * u : 2 * u + 2, :],
                    in_=w[256 * u : 256 * (u + 1), :].rearrange("(q e) k -> q e k", e=2),
                )

        nc.scalar.activation(out=warm[:], in_=warm[:], func=ACT.Silu)

        own_limb = keep.tile([P, LIMBS], F32, name="own_limb")
        nc.vector.tensor_reduce(
            out=own_limb[:], in_=ident[:].rearrange("p (a j) -> p j a", j=LIMBS), axis=AXIS_X, op=ALU.add
        )
        own_group = keep.tile([P, GROUPS], F32, name="own_group")
        nc.vector.tensor_reduce(
            out=own_group[:], in_=ident[:].rearrange("p (a j) -> p a j", j=LIMBS), axis=AXIS_X, op=ALU.add
        )
        PAIRS = 1 + LIMBS
        diag_flat = keep.tile([P, LIMBS * (PAIRS + 1)], F32, name="diag_flat")
        nc.vector.memset(diag_flat[:], 0.0)
        nc.vector.memset(diag_flat[:].rearrange("p (i s) -> p i s", s=PAIRS + 1)[:, :, 1], 2.0)
        two_on_diag = diag_flat[:, 0 : LIMBS * PAIRS].rearrange("p (i s) -> p i s", s=PAIRS)
        nc.vector.tensor_scalar(out=two_on_diag[:, :, 0], in0=own_limb[:], scalar1=2.0, scalar2=None, op0=ALU.mult)
        twice_r = keep.tile([P, LIMBS, PAIRS + 1], F32, name="twice_r")
        nc.vector.memset(twice_r[:, :, PAIRS], 2.0e-6)

        PLANES = 2 * COORDS
        THR = PLANES * LIMBS
        comb = keep.tile([P, 64], BF16, name="comb")
        nc.vector.memset(comb[:], 0.0)
        unit = ident[:, 0:N_POS].rearrange("k (i c) -> k c i", c=COORDS)
        planes = comb[:, 0:THR].rearrange("k (g c i) -> k g c i", g=2, c=COORDS)
        for g, op in enumerate((ALU.add, ALU.subtract)):
            nc.vector.tensor_tensor(out=planes[:, g, 0:2, :], in0=unit[:, 0:2, :], in1=unit[:, 1:3, :], op=op)
            nc.vector.tensor_tensor(out=planes[:, g, 2, :], in0=unit[:, 2, :], in1=unit[:, 0, :], op=op)
        nc.vector.tensor_copy(out=comb[:, THR : THR + 1], in_=ident[:, N_POS : N_POS + 1])
        combos = psum.tile([P, BANK], F32, tag="bank", name="combos")
        nc.tensor.matmul(
            out=combos[:, 0:64], lhsT=small_col[:, 0:1].to_broadcast([P, P]), rhs=comb[:], start=True, stop=True
        )
        turns = keep.tile([P, PLANES, LIMBS], F32, name="turns")
        nc.vector.tensor_scalar(
            out=turns[:].rearrange("p w i -> p (w i)"),
            in0=combos[:, 0:THR],
            scalar1=1.0 / (4.0 * math.pi),
            scalar2=None,
            op0=ALU.mult,
        )
        minus_thr = keep.tile([P, 1], F32, name="minus_thr")
        nc.vector.tensor_scalar(
            out=minus_thr[:], in0=combos[:, THR : THR + 1], scalar1=-1.0, scalar2=None, op0=ALU.mult
        )
        pair_shape = [P, PLANES, LIMBS, LIMBS]
        mid = keep.tile(pair_shape, F32, name="mid")
        nc.vector.tensor_tensor(
            out=mid[:],
            in0=turns[:].unsqueeze(3).to_broadcast(pair_shape),
            in1=turns[:].unsqueeze(2).to_broadcast(pair_shape),
            op=ALU.add,
        )
        whole = keep.tile(pair_shape, F32, name="whole")
        nc.vector.tensor_scalar(
            out=whole[:], in0=mid[:], scalar1=ROUND_MAGIC, scalar2=ROUND_MAGIC, op0=ALU.add, op1=ALU.subtract
        )
        frac = keep.tile(pair_shape, F32, name="frac")
        nc.vector.tensor_tensor(out=frac[:], in0=mid[:], in1=whole[:], op=ALU.subtract)

        b_route_f = keep.tile([P, SLOTS], F32, name="b_route_f")
        nc.gpsimd.tensor_copy(out=b_route_f[:], in_=b_route_bf[:].rearrange("q u e -> q (u e)"))
        half_b_gate = keep.tile([P, SLOTS], F32, name="half_b_gate")
        nc.gpsimd.tensor_scalar(
            out=half_b_gate[:],
            in0=b_gate_bf[:].rearrange("q u e -> q (u e)"),
            scalar1=0.5,
            scalar2=0.0,
            op0=ALU.mult,
            op1=ALU.add,
        )

        x_grouped = keep.tile([P, TOKENS, SLOTS], BF16, name="x_grouped", align_bytes=64)
        x_codes = keep.tile([P, TOKENS], U32, name="x_codes", align_bytes=64)
        x_scales = keep.tile([P, TOKENS], U8, name="x_scales", align_bytes=64)
        wr_grouped = [keep.tile([P, HALF, SLOTS], BF16, name="wr_grouped%d" % u, align_bytes=64) for u in range(2)]
        wr_codes = keep.tile([P, H], U32, name="wr_codes", align_bytes=64)
        wr_scales = keep.tile([P, H], U8, name="wr_scales", align_bytes=64)

        transpose_and_group(nc, psum, ident[:], [x_sb[:, n, :] for n in range(TOKEN_TILES)], x_grouped[:], False)
        sines = keep.tile([P, PLANES, LIMBS * LIMBS], F32, name="sines")
        nc.scalar.activation(
            out=sines[:].rearrange("p w n -> p (w n)"),
            in_=frac[:].rearrange("p w i j -> p (w i j)"),
            func=ACT.Sin,
            scale=2.0 * math.pi,
        )
        for u in range(2):
            transpose_and_group(nc, psum, ident[:], [wr_sb[:, 2 * u + e, :] for e in range(2)], wr_grouped[u][:], True)

        b_route_t = psum.tile([P, SLOTS, P], F32, tag="bank", name="b_route_t")
        for s in range(SLOTS):
            nc.tensor.transpose(b_route_t[:, s, :], b_route_f[:, s : s + 1].to_broadcast([P, P]), ident[:])
        b_route_rows = keep.tile([P, SLOTS, P], F32, name="b_route_rows")
        nc.scalar.copy(out=b_route_rows[:], in_=b_route_t[:])

        gyroid = keep.tile([P, LIMBS, PAIRS], F32, name="gyroid")
        nc.vector.tensor_reduce(
            out=gyroid[:, :, 1:PAIRS],
            in_=sines[:].rearrange("p w (i j) -> p i j w", j=LIMBS),
            axis=AXIS_X,
            op=ALU.add,
        )
        quantise(nc, x_grouped[:], x_codes[:], x_scales[:])
        picked = keep.tile([P, LIMBS, LIMBS], F32, name="picked")
        nc.vector.tensor_tensor(
            out=picked[:],
            in0=gyroid[:, :, 1:PAIRS],
            in1=own_limb[:].unsqueeze(1).to_broadcast([P, LIMBS, LIMBS]),
            op=ALU.mult,
        )
        quantise(nc, wr_grouped[0][:], wr_codes[:, 0:HALF], wr_scales[:, 0:HALF])
        nc.vector.tensor_reduce(out=gyroid[:, :, 0], in_=picked[:], axis=AXIS_X, op=ALU.add)
        tanh_f = keep.tile([P, LIMBS, PAIRS], F32, name="tanh_f")
        nc.scalar.activation(out=tanh_f[:], in_=gyroid[:], func=ACT.Tanh, scale=0.5, bias=minus_thr[:, 0:1])
        quantise(nc, wr_grouped[1][:], wr_codes[:, HALF:H], wr_scales[:, HALF:H])

        wg_parts = [(u, g) for u in range(2) for g in range(2)]
        wg_grouped = {
            part: keep.tile([P, HALF, SLOTS], BF16, name="wg_grouped%d%d" % part, align_bytes=64) for part in wg_parts
        }
        wg_codes = [keep.tile([P, H], U32, name="wg_codes%d" % g, align_bytes=64) for g in range(2)]
        wg_scales = [keep.tile([P, H], U8, name="wg_scales%d" % g, align_bytes=64) for g in range(2)]

        def group_w_gate(u, g):
            rows = [wg_sb[:, 2 * u + e, g * H : (g + 1) * H] for e in range(2)]
            transpose_and_group(nc, psum, ident[:], rows, wg_grouped[(u, g)][:], True)

        for part in wg_parts[0:2]:
            group_w_gate(*part)

        proj_ps = [psum.tile([P, BANK], F32, tag="bank", name="proj_ps%d" % n) for n in range(TOKEN_TILES)]
        projected = [keep.tile([P, SLOTS, P], F32, name="projected%d" % n) for n in range(TOKEN_TILES)]
        for n in range(TOKEN_TILES):
            tokens = slice(n * P, (n + 1) * P)
            for u in range(2):
                cols = slice(u * HALF, (u + 1) * HALF)
                nc.tensor.matmul_mx(
                    out=proj_ps[n][:, cols],
                    lhsT=x_codes[:, tokens].bitcast(FP8X4),
                    lhsT_scale=x_scales[:, tokens],
                    rhs=wr_codes[:, cols].bitcast(FP8X4),
                    rhs_scale=wr_scales[:, cols],
                    start=True,
                    stop=True,
                )

        def add_b_route(n, u):
            cols = slice(u * HALF, (u + 1) * HALF)
            nc.vector.tensor_tensor(
                out=projected[n][:].rearrange("t s q -> t (s q)")[:, cols],
                in0=proj_ps[n][:, cols],
                in1=b_route_rows[:].rearrange("t s q -> t (s q)")[:, cols],
                op=ALU.add,
            )

        nc.vector.scalar_tensor_tensor(
            out=twice_r[:, :, 0:PAIRS], in0=tanh_f[:], scalar=1.0, in1=two_on_diag, op0=ALU.add, op1=ALU.max
        )
        add_b_route(0, 0)
        row_sum = keep.tile([P, LIMBS], F32, name="row_sum")
        nc.vector.tensor_reduce(out=row_sum[:], in_=twice_r[:, :, 1 : PAIRS + 1], axis=AXIS_X, op=ALU.add)
        add_b_route(0, 1)
        row_inv = keep.tile([P, LIMBS], F32, name="row_inv")
        nc.vector.reciprocal(out=row_inv[:], in_=row_sum[:])
        to_limb = keep.tile([P, LIMBS], F32, name="to_limb")
        nc.vector.tensor_tensor(out=to_limb[:], in0=twice_r[:, :, 0], in1=row_inv[:], op=ALU.mult)
        mixer = keep.tile([P, GROUPS, LIMBS], F32, name="mixer")
        nc.vector.tensor_tensor(
            out=mixer[:],
            in0=own_group[:].unsqueeze(2).to_broadcast([P, GROUPS, LIMBS]),
            in1=to_limb[:].unsqueeze(1).to_broadcast([P, GROUPS, LIMBS]),
            op=ALU.mult,
        )
        for u in range(2):
            add_b_route(1, u)

        for part in wg_parts[2:4]:
            group_w_gate(*part)
        for u, g in wg_parts:
            cols = slice(u * HALF, (u + 1) * HALF)
            quantise(nc, wg_grouped[(u, g)][:], wg_codes[g][:, cols], wg_scales[g][:, cols])

        r_codes = keep.tile([P, TOKENS], U32, name="r_codes", align_bytes=64)
        r_scales = keep.tile([P, TOKENS], U8, name="r_scales", align_bytes=64)
        diff = [keep.tile([P, SLOTS, P], F32, name="diff%d" % n) for n in range(TOKEN_TILES)]
        for n in range(TOKEN_TILES):
            tokens = slice(n * P, (n + 1) * P)
            routed_ps = psum.tile([P, SLOTS, P], F32, tag="bank", name="routed_ps")
            for s in range(SLOTS):
                nc.tensor.matmul(
                    out=routed_ps[:, s, :],
                    lhsT=projected[n][:, s, :],
                    rhs=mixer[:].rearrange("t a i -> t (a i)"),
                    start=True,
                    stop=True,
                )
            r_grouped = keep.tile([P, P, SLOTS], BF16, name="r_grouped%d" % n, align_bytes=64)
            nc.scalar.copy(out=r_grouped[:], in_=routed_ps[:].rearrange("q s t -> q t s"))
            quantise(nc, r_grouped[:], r_codes[:, tokens], r_scales[:, tokens])
            nc.vector.tensor_tensor(
                out=diff[n][:],
                in0=routed_ps[:],
                in1=x_grouped[:, tokens, :].rearrange("q t s -> q s t"),
                op=ALU.subtract,
            )

        tanh_g = [keep.tile([P, SLOTS, P], F32, name="tanh_g%d" % n) for n in range(TOKEN_TILES)]
        for n in range(TOKEN_TILES):
            tokens = slice(n * P, (n + 1) * P)
            gate_ps = [psum.tile([P, P], F32, tag="bank", name="gate_ps%d" % s) for s in range(SLOTS)]
            for g, (codes, scales) in enumerate(((x_codes, x_scales), (r_codes, r_scales))):
                for s in range(SLOTS):
                    feats = slice(s * P, (s + 1) * P)
                    nc.tensor.matmul_mx(
                        out=gate_ps[s][:],
                        lhsT=wg_codes[g][:, feats].bitcast(FP8X4),
                        lhsT_scale=wg_scales[g][:, feats],
                        rhs=codes[:, tokens].bitcast(FP8X4),
                        rhs_scale=scales[:, tokens],
                        start=(g == 0),
                        stop=(g == 1),
                    )
            for s in range(SLOTS):
                nc.scalar.activation(
                    out=tanh_g[n][:, s, :],
                    in_=gate_ps[s][:],
                    func=ACT.Tanh,
                    scale=0.5,
                    bias=half_b_gate[:, s : s + 1],
                )

        units = [(n, u) for n in range(TOKEN_TILES) for u in range(2)]
        moved_t = {}

        def weigh_and_transpose(n, u):
            moved = keep.tile([P, 2, P], F32, name="moved%d%d" % (n, u))
            nc.vector.scalar_tensor_tensor(
                out=moved[:].rearrange("q e t -> q (e t)"),
                in0=tanh_g[n][:, 2 * u : 2 * u + 2, :].rearrange("q e t -> q (e t)"),
                scalar=1.0,
                in1=diff[n][:, 2 * u : 2 * u + 2, :].rearrange("q e t -> q (e t)"),
                op0=ALU.add,
                op1=ALU.mult,
            )
            moved_t[(n, u)] = psum.tile([P, 2, P], F32, tag="bank", name="moved_t")
            for e in range(2):
                nc.tensor.transpose(moved_t[(n, u)][:, e, :], moved[:, e, :], ident[:])

        def add_x_and_store(n, u):
            feats = slice(u * HALF, (u + 1) * HALF)
            out_sb = keep.tile([P, HALF], F32, name="out_sb%d%d" % (n, u))
            nc.vector.scalar_tensor_tensor(
                out=out_sb[:].rearrange("t (q e) -> t q e", e=2),
                in0=moved_t[(n, u)][:].rearrange("t e q -> t q e"),
                scalar=0.5,
                in1=x_sb[:, n, feats].rearrange("t (q e) -> t q e", e=2),
                op0=ALU.mult,
                op1=ALU.add,
            )
            nc.sync.dma_start(out=out_rows[n * P : (n + 1) * P, feats], in_=out_sb[:])

        for unit in units:
            weigh_and_transpose(*unit)
        for unit in units:
            add_x_and_store(*unit)
